import numpy as np
import ml_dtypes


def mxq(x, axis, fmt="e4m3"):
    dtype, down = {"e4m3": (ml_dtypes.float8_e4m3fn, 7), "e5m2": (ml_dtypes.float8_e5m2, 14)}[fmt]
    v = np.moveaxis(np.asarray(x, np.float32).astype(ml_dtypes.bfloat16).astype(np.float64), axis, -1)
    blocks = v.reshape(v.shape[:-1] + (-1, 32))
    amax = np.abs(blocks).max(-1, keepdims=True)
    byte = np.maximum(np.where(amax > 0, np.frexp(amax)[1] - 1 + 127, 0) - down, 1)
    scale = np.exp2(byte - 127.0)
    codes = (blocks / scale).astype(np.float32).astype(dtype).astype(np.float64)
    return np.moveaxis((codes * scale).reshape(v.shape), -1, axis)


WIDE = False


def mx_kscale(k):
    if not WIDE:
        return np.ones(k)
    levels = np.array([10, -10, 5, -5, 0])
    a = np.random.permutation(np.resize(levels, k // 512 * 4)).reshape(k // 512, 4)
    idx = np.arange(k)
    return np.exp2(a[idx // 512, idx % 128 // 32])


BF16 = ml_dtypes.bfloat16


def bf(x):
    return np.asarray(x, np.float32).astype(BF16)


def f64(x):
    return np.asarray(x).astype(np.float64)


E2M1 = np.array([0.0, 0.5, 1.0, 1.5, 2.0, 3.0, 4.0, 6.0, -0.0, -0.5, -1.0, -1.5, -2.0, -3.0, -4.0, -6.0])


def pack_weight(w, fmt):
    k, n = w.shape
    w = f64(bf(w)).reshape(k // 32, 32, n)
    amax = np.abs(w).max(1)
    if fmt == "e4m3":
        byte = np.frexp(amax)[1] - 1 + 127 - 7
    else:
        mant, ex = np.frexp(amax / 6.0)
        byte = np.where(mant > 0.5, ex, ex - 1) + 127
    byte = np.clip(np.where(amax > 0, byte, 1), 1, 254)
    scaled = (w * np.exp2(127.0 - byte)[:, None, :]).reshape(k, n).astype(np.float32)
    by_word = np.ascontiguousarray(scaled.reshape(k // 512, 128, 4, n).transpose(0, 1, 3, 2))
    if fmt == "e4m3":
        words = by_word.astype(ml_dtypes.float8_e4m3fn).view(np.uint8)
    else:
        c = by_word.astype(ml_dtypes.float4_e2m1fn).view(np.uint8) & 0xF
        words = c[..., 0::2] | (c[..., 1::2] << 4)
    return np.ascontiguousarray(words), np.ascontiguousarray(byte.astype(np.uint8).reshape(k // 512, 16, n))


def unpack_weight(words, scales, fmt):
    g, p, n, _ = words.shape
    if fmt == "e4m3":
        vals = np.ascontiguousarray(words).view(ml_dtypes.float8_e4m3fn).astype(np.float64)
    else:
        nib = np.empty((g, p, n, 4), np.uint8)
        nib[..., 0::2] = words & 0xF
        nib[..., 1::2] = words >> 4
        vals = E2M1[nib]
    vals = vals * np.repeat(np.exp2(scales.astype(np.float64) - 127.0), 8, axis=1)[..., None]
    return vals.transpose(0, 1, 3, 2).reshape(g * 512, n)

def pack4(w):
    words, scales = pack_weight(w, "e2m1")
    return words.reshape(words.shape[0], 128, -1), scales


def unpack4(words, scales):
    return unpack_weight(words.reshape(words.shape[0], 128, -1, 2), scales, "e2m1")


B, T, E, H, FF = 4, 1024, 1024, 8, 512
EPS = 1e-5


def layernorm(r, g):
    mu = r.mean(-1, keepdims=True)
    var = ((r - mu) ** 2).mean(-1, keepdims=True)
    return (r - mu) / np.sqrt(var + EPS) * g


def setup_inputs():
    t = mx_kscale(FF)
    z = np.random.standard_normal((B, T, FF))
    y_act = bf(z * z / (1.0 + np.exp(-z)) * t)
    h = bf(np.random.standard_normal((B, T, E)))
    W2_words, W2_scales = pack4(np.random.standard_normal((FF, E)) / np.sqrt(FF) / t[:, None])
    return {
        "y_act": y_act,
        "h": h,
        "W2_words": W2_words,
        "W2_scales": W2_scales,
        "b2": bf(np.random.standard_normal(E) * 0.1),
        "g2": bf(1.0 + np.random.standard_normal(E) * 0.1),
    }


def reference(y_act, h, W2_words, W2_scales, b2, g2):
    ff = (mxq(f64(y_act), 2, "e4m3") @ unpack4(W2_words, W2_scales)) + f64(b2)
    return layernorm(ff + f64(h), f64(g2))

@@ -1,0 +1,254 @@
+from contextlib import ExitStack
+
+import concourse.mybir as mybir
+from concourse.masks import make_identity
+
+F32 = mybir.dt.float32
+BF16 = mybir.dt.bfloat16
+I32 = mybir.dt.int32
+U32 = mybir.dt.uint32
+U8 = mybir.dt.uint8
+FP8X4 = mybir.dt.float8_e4m3fn_x4
+FP4X4 = mybir.dt.float4_e2m1fn_x4
+ALU = mybir.AluOpType
+ACT = mybir.ActivationFunctionType
+
+P = 128
+TOKENS = 4096
+K = 512
+E = 1024
+BANK = 512
+HALVES = E // BANK
+PAIR = 2
+N_TILES = TOKENS // P
+N_PAIRS = N_TILES // PAIR
+PREFETCH = 2
+EPS = 1e-5
+
+FLOPS = 2 * TOKENS * K * E
+
+
+def tile_transformerblock_pb_t_kernel(tc, y_act, h, W2_words, W2_scales, b2, g2, out):
+    nc = tc.nc
+
+    y_pairs = y_act.flatten_outer_dims().rearrange("(q p j) k -> q p j k", p=P, j=PAIR)
+    h_pairs = h.flatten_outer_dims().rearrange("(q p j) e -> q p j e", p=P, j=PAIR)
+    out_pairs = out.flatten_outer_dims().rearrange("(q p j) e -> q p j e", p=P, j=PAIR)
+
+    with ExitStack() as ctx:
+        ctx.enter_context(tc.manual_schedule())
+        const = ctx.enter_context(tc.tile_pool(name="const", bufs=1))
+        loads = ctx.enter_context(tc.tile_pool(name="loads", bufs=4))
+        quant = ctx.enter_context(tc.tile_pool(name="quant", bufs=2))
+        work = ctx.enter_context(tc.tile_pool(name="work", bufs=4))
+        stats = ctx.enter_context(tc.tile_pool(name="stats", bufs=4))
+        psum_g2 = ctx.enter_context(tc.psum_pool(name="psum_g2", bufs=1))
+        psum_yt = ctx.enter_context(tc.psum_pool(name="psum_yt", bufs=2))
+        psum_mm = ctx.enter_context(tc.psum_pool(name="psum_mm", bufs=2))
+
+        b2_rows = const.tile([P, E], BF16)
+        g2_rows = const.tile([P, E], BF16)
+        w_scales = const.tile([P, E], U8, align_bytes=64)
+        w_words = const.tile([P, 2 * E], U8, align_bytes=64)
+        ones = const.tile([P, P], BF16)
+        eps = const.tile([P, 1], F32)
+        table_warm = const.tile([P, 1], F32)
+        ident = const.tile([P, P], F32)
+        b2_all = const.tile([P, E], F32)
+
+        nc.vector.memset(b2_rows[:].bitcast(I32), 0)
+        nc.vector.memset(w_scales[:].bitcast(I32), 0)
+        nc.vector.memset(g2_rows[:].bitcast(I32), 0)
+        nc.vector.memset(ones[:], 1.0)
+        nc.vector.memset(eps[:], EPS)
+        make_identity(nc, ident[:])
+
+        nc.scalar.dma_start(out=b2_rows[0:1, :], in_=b2.unsqueeze(0))
+        nc.scalar.dma_start(out=g2_rows[0:1, :], in_=g2.unsqueeze(0))
+        nc.scalar.activation(out=table_warm[:], in_=eps[:], func=ACT.Sqrt)
+
+        y_sb = {}
+        h_sb = {}
+
+        def load_pair(q):
+            y_sb[q] = loads.tile([P, PAIR, K], BF16, name="y_sb")
+            nc.sync.dma_start(out=y_sb[q][:], in_=y_pairs[q])
+            h_sb[q] = loads.tile([P, PAIR, E], BF16, name="h_sb")
+            nc.sync.dma_start(out=h_sb[q][:], in_=h_pairs[q])
+
+        load_pair(0)
+        nc.sync.dma_start(out=w_words[:].bitcast(I32), in_=W2_words[0].bitcast(I32))
+        for quadrant in range(4):
+            nc.sync.dma_start(
+                out=w_scales[32 * quadrant : 32 * quadrant + 4, :].bitcast(I32),
+                in_=W2_scales[0, 4 * quadrant : 4 * quadrant + 4, :].bitcast(I32),
+            )
+        for q in range(1, PREFETCH):
+            load_pair(q)
+
+        def spread_over_partitions(rows, banks):
+            for c in range(HALVES):
+                nc.tensor.matmul(
+                    out=banks[c][:],
+                    lhsT=ones[:],
+                    rhs=rows[:, c * BANK : (c + 1) * BANK],
+                    start=True,
+                    stop=True,
+                )
+
+        b2_ps = [psum_mm.tile([P, BANK], F32, name="mm%d" % c) for c in range(HALVES)]
+        spread_over_partitions(b2_rows, b2_ps)
+        nc.scalar.copy(out=b2_all[:, 0:BANK], in_=b2_ps[0][:])
+        nc.vector.tensor_copy(out=b2_all[:, BANK:E], in_=b2_ps[1][:])
+        g2_ps = [psum_g2.tile([P, BANK], F32, name="g2_ps%d" % c) for c in range(HALVES)]
+
+        y_t = {}
+        grouped = {}
+        y_codes = {}
+        y_scales = {}
+        mm = {}
+        hb = {}
+        r = {}
+        z = {}
+        sums = {}
+        neg_mean = {}
+        ssq = {}
+        std = {}
+        rstd = {}
+
+        def transpose_pair(q):
+            y_t[q] = psum_yt.tile([P, PAIR, 2, P], F32, name="y_t")
+            words = y_sb[q][:].rearrange("p j k -> p (j k)").bitcast(F32)
+            for j in range(PAIR):
+                for u in range(2):
+                    first = j * (K // 2) + u
+                    nc.tensor.transpose(
+                        out=y_t[q][:, j, u, :],
+                        in_=words[:, first : (j + 1) * (K // 2) : 2],
+                        identity=ident[:],
+                    )
+
+        def group_pair(q):
+            grouped[q] = quant.tile([P, PAIR * P * 4], BF16, name="grouped", align_bytes=64)
+            nc.scalar.copy(
+                out=grouped[q][:].bitcast(F32).rearrange("p (j i u) -> p j i u", j=PAIR, u=2),
+                in_=y_t[q][:].rearrange("p j u i -> p j i u"),
+            )
+
+        def quantise_pair(q):
+            y_codes[q] = quant.tile([P, PAIR * P], U32, name="y_codes", align_bytes=64)
+            y_scales[q] = quant.tile([P, PAIR * P], U8, name="y_scales", align_bytes=64)
+            nc.vector.quantize_mx(
+                out=y_codes[q][:].bitcast(FP8X4), scales=y_scales[q][:], in_=grouped[q][:]
+            )
+
+        def multiply(i):
+            q, j = divmod(i, PAIR)
+            tokens = slice(j * P, (j + 1) * P)
+            mm[i] = [psum_mm.tile([P, BANK], F32, name="mm%d" % c) for c in range(HALVES)]
+            for c in range(HALVES):
+                nc.tensor.matmul_mx(
+                    out=mm[i][c][:],
+                    lhsT=y_codes[q][:, tokens].bitcast(FP8X4),
+                    lhsT_scale=y_scales[q][:, tokens],
+                    rhs=w_words[:, c * 2 * BANK : (c + 1) * 2 * BANK].bitcast(FP4X4),
+                    rhs_scale=w_scales[:, c * BANK : (c + 1) * BANK],
+                    start=True,
+                    stop=True,
+                )
+
+        def add_bias(i):
+            q, j = divmod(i, PAIR)
+            hb[i] = work.tile([P, E], F32, name="hb")
+            nc.gpsimd.tensor_tensor(out=hb[i][:], in0=h_sb[q][:, j, :], in1=b2_all[:], op=ALU.add)
+
+        def add_residual(i):
+            r[i] = work.tile([P, E], F32, name="r")
+            sums[i] = stats.tile([P, HALVES], F32, name="sums")
+            for c in range(HALVES):
+                cols = slice(c * BANK, (c + 1) * BANK)
+                nc.vector.scalar_tensor_tensor(
+                    out=r[i][:, cols],
+                    in0=mm[i][c][:],
+                    scalar=1.0,
+                    in1=hb[i][:, cols],
+                    op0=ALU.mult,
+                    op1=ALU.add,
+                    accum_out=sums[i][:, c : c + 1],
+                )
+
+        def mean(i):
+            neg_mean[i] = stats.tile([P, 1], F32, name="neg_mean")
+            nc.vector.tensor_scalar(
+                out=neg_mean[i][:],
+                in0=sums[i][:, 0:1],
+                scalar1=sums[i][:, 1:2],
+                scalar2=-1.0 / E,
+                op0=ALU.add,
+                op1=ALU.mult,
+            )
+
+        def squares(i):
+            scratch = work.tile([P, E], BF16, name="scratch")
+            ssq[i] = stats.tile([P, 1], F32, name="ssq")
+            nc.scalar.activation(
+                out=scratch[:],
+                in_=r[i][:],
+                func=ACT.Square,
+                bias=neg_mean[i][:, 0:1],
+                scale=1.0,
+                accum_out=ssq[i][:],
+            )
+            std[i] = stats.tile([P, 1], F32, name="std")
+            nc.scalar.activation(
+                out=std[i][:], in_=ssq[i][:], func=ACT.Sqrt, bias=eps[:, 0:1], scale=1.0 / E
+            )
+
+        def centre_and_gain(i):
+            z[i] = work.tile([P, E], F32, name="z")
+            for c in range(HALVES):
+                cols = slice(c * BANK, (c + 1) * BANK)
+                nc.vector.scalar_tensor_tensor(
+                    out=z[i][:, cols],
+                    in0=r[i][:, cols],
+                    scalar=neg_mean[i][:, 0:1],
+                    in1=g2_ps[c][:],
+                    op0=ALU.add,
+                    op1=ALU.mult,
+                )
+
+        def reciprocal(i):
+            rstd[i] = stats.tile([P, 1], F32, name="rstd")
+            nc.vector.reciprocal(out=rstd[i][:], in_=std[i][:])
+
+        def scale_and_store(i):
+            q, j = divmod(i, PAIR)
+            nc.scalar.activation(out=z[i][:], in_=z[i][:], func=ACT.Copy, scale=rstd[i][:, 0:1])
+            nc.sync.dma_start(out=out_pairs[q][:, j, :], in_=z[i][:])
+
+        def for_tile(stage, i):
+            if 0 <= i < N_TILES:
+                stage(i)
+
+        def for_pair(stage, first_tile):
+            if first_tile % PAIR == 0 and 0 <= first_tile < N_TILES:
+                stage(first_tile // PAIR)
+
+        def step(t):
+            for_pair(load_pair, t + 4 + PAIR * PREFETCH)
+            for_pair(transpose_pair, t + 4)
+            for_pair(group_pair, t + 3)
+            for_pair(quantise_pair, t + 2)
+            for_tile(add_bias, t + 2)
+            for_tile(multiply, t + 1)
+            for_tile(add_residual, t)
+            for_tile(centre_and_gain, t - 1)
+            for_tile(mean, t)
+            for_tile(squares, t - 1)
+            for_tile(reciprocal, t - 1)
+            for_tile(scale_and_store, t - 2)
+
+        step(-4)
+        spread_over_partitions(g2_rows, g2_ps)
+        for t in range(-3, N_TILES + 2):
+            step(t)

@@ -178,14 +178,16 @@ def tile_transformerblock_pb_t_kernel(tc, y_act, h, W2_words, W2_scales, b2, g2,
                 )
 
         def mean(i):
+            scaled_sums = stats.tile([P, HALVES], F32, name="scaled_sums")
             neg_mean[i] = stats.tile([P, 1], F32, name="neg_mean")
             nc.vector.tensor_scalar(
-                out=neg_mean[i][:],
-                in0=sums[i][:, 0:1],
-                scalar1=sums[i][:, 1:2],
-                scalar2=-1.0 / E,
-                op0=ALU.add,
-                op1=ALU.mult,
+                out=scaled_sums[:],
+                in0=sums[i][:],
+                scalar1=-1.0 / E,
+                scalar2=None,
+                op0=ALU.mult,
+                op1=ALU.add,
+                accum_out=neg_mean[i][:],
             )
 
         def squares(i):

@@ -65,7 +65,7 @@ def tile_transformerblock_pb_t_kernel(tc, y_act, h, W2_words, W2_scales, b2, g2,
 
         nc.scalar.dma_start(out=b2_rows[0:1, :], in_=b2.unsqueeze(0))
         nc.scalar.dma_start(out=g2_rows[0:1, :], in_=g2.unsqueeze(0))
-        nc.scalar.activation(out=table_warm[:], in_=eps[:], func=ACT.Sqrt)
+        nc.scalar.activation(out=table_warm[:], in_=eps[:], func=ACT.Abs_reciprocal_sqrt)
 
         y_sb = {}
         h_sb = {}
@@ -113,7 +113,6 @@ def tile_transformerblock_pb_t_kernel(tc, y_act, h, W2_words, W2_scales, b2, g2,
         sums = {}
         neg_mean = {}
         ssq = {}
-        std = {}
         rstd = {}
 
         def transpose_pair(q):
@@ -201,10 +200,6 @@ def tile_transformerblock_pb_t_kernel(tc, y_act, h, W2_words, W2_scales, b2, g2,
                 scale=1.0,
                 accum_out=ssq[i][:],
             )
-            std[i] = stats.tile([P, 1], F32, name="std")
-            nc.scalar.activation(
-                out=std[i][:], in_=ssq[i][:], func=ACT.Sqrt, bias=eps[:, 0:1], scale=1.0 / E
-            )
 
         def centre_and_gain(i):
             z[i] = work.tile([P, E], F32, name="z")
@@ -219,9 +214,15 @@ def tile_transformerblock_pb_t_kernel(tc, y_act, h, W2_words, W2_scales, b2, g2,
                     op1=ALU.mult,
                 )
 
-        def reciprocal(i):
+        def inverse_std(i):
             rstd[i] = stats.tile([P, 1], F32, name="rstd")
-            nc.vector.reciprocal(out=rstd[i][:], in_=std[i][:])
+            nc.scalar.activation(
+                out=rstd[i][:],
+                in_=ssq[i][:],
+                func=ACT.Abs_reciprocal_sqrt,
+                bias=eps[:, 0:1],
+                scale=1.0 / E,
+            )
 
         def scale_and_store(i):
             q, j = divmod(i, PAIR)
@@ -247,8 +248,8 @@ def tile_transformerblock_pb_t_kernel(tc, y_act, h, W2_words, W2_scales, b2, g2,
             for_tile(centre_and_gain, t - 1)
             for_tile(mean, t)
             for_tile(squares, t - 1)
-            for_tile(reciprocal, t - 1)
             for_tile(scale_and_store, t - 2)
+            for_tile(inverse_std, t - 1)
 
         step(-4)
         spread_over_partitions(g2_rows, g2_ps)

@@ -168,9 +168,9 @@ def tile_transformerblock_pb_t_kernel(tc, y_act, h, W2_words, W2_scales, b2, g2,
                 cols = slice(c * BANK, (c + 1) * BANK)
                 nc.vector.scalar_tensor_tensor(
                     out=r[i][:, cols],
-                    in0=mm[i][c][:],
+                    in0=hb[i][:, cols],
                     scalar=1.0,
-                    in1=hb[i][:, cols],
+                    in1=mm[i][c][:],
                     op0=ALU.mult,
                     op1=ALU.add,
                     accum_out=sums[i][:, c : c + 1],

@@ -23,6 +23,8 @@ PAIR = 2
 N_TILES = TOKENS // P
 N_PAIRS = N_TILES // PAIR
 PREFETCH = 2
+BIAS_ON_GPSIMD = 768
+BIAS_ON_VECTOR = E - BIAS_ON_GPSIMD
 EPS = 1e-5
 
 FLOPS = 2 * TOKENS * K * E
@@ -43,7 +45,8 @@ def tile_transformerblock_pb_t_kernel(tc, y_act, h, W2_words, W2_scales, b2, g2,
         work = ctx.enter_context(tc.tile_pool(name="work", bufs=4))
         stats = ctx.enter_context(tc.tile_pool(name="stats", bufs=4))
         psum_g2 = ctx.enter_context(tc.psum_pool(name="psum_g2", bufs=1))
-        psum_yt = ctx.enter_context(tc.psum_pool(name="psum_yt", bufs=2))
+        psum_b2 = ctx.enter_context(tc.psum_pool(name="psum_b2", bufs=1))
+        psum_yt = ctx.enter_context(tc.psum_pool(name="psum_yt", bufs=1))
         psum_mm = ctx.enter_context(tc.psum_pool(name="psum_mm", bufs=2))
 
         b2_rows = const.tile([P, E], BF16)
@@ -54,7 +57,7 @@ def tile_transformerblock_pb_t_kernel(tc, y_act, h, W2_words, W2_scales, b2, g2,
         eps = const.tile([P, 1], F32)
         table_warm = const.tile([P, 1], F32)
         ident = const.tile([P, P], F32)
-        b2_all = const.tile([P, E], F32)
+        b2_head = const.tile([P, BIAS_ON_GPSIMD], F32)
 
         nc.vector.memset(b2_rows[:].bitcast(I32), 0)
         nc.vector.memset(w_scales[:].bitcast(I32), 0)
@@ -86,20 +89,20 @@ def tile_transformerblock_pb_t_kernel(tc, y_act, h, W2_words, W2_scales, b2, g2,
         for q in range(1, PREFETCH):
             load_pair(q)
 
-        def spread_over_partitions(rows, banks):
-            for c in range(HALVES):
-                nc.tensor.matmul(
-                    out=banks[c][:],
-                    lhsT=ones[:],
-                    rhs=rows[:, c * BANK : (c + 1) * BANK],
-                    start=True,
-                    stop=True,
-                )
+        def spread_over_partitions(rows, first, bank):
+            width = bank.shape[1]
+            nc.tensor.matmul(
+                out=bank[:], lhsT=ones[:], rhs=rows[:, first : first + width], start=True, stop=True
+            )
 
-        b2_ps = [psum_mm.tile([P, BANK], F32, name="mm%d" % c) for c in range(HALVES)]
-        spread_over_partitions(b2_rows, b2_ps)
-        nc.scalar.copy(out=b2_all[:, 0:BANK], in_=b2_ps[0][:])
-        nc.vector.tensor_copy(out=b2_all[:, BANK:E], in_=b2_ps[1][:])
+        b2_ps0 = psum_mm.tile([P, BANK], F32, name="mm0")
+        b2_ps1 = psum_mm.tile([P, BIAS_ON_GPSIMD - BANK], F32, name="mm1")
+        b2_tail = psum_b2.tile([P, BIAS_ON_VECTOR], F32)
+        spread_over_partitions(b2_rows, 0, b2_ps0)
+        spread_over_partitions(b2_rows, BANK, b2_ps1)
+        spread_over_partitions(b2_rows, BIAS_ON_GPSIMD, b2_tail)
+        nc.scalar.copy(out=b2_head[:, 0:BANK], in_=b2_ps0[:])
+        nc.vector.tensor_copy(out=b2_head[:, BANK:BIAS_ON_GPSIMD], in_=b2_ps1[:])
         g2_ps = [psum_g2.tile([P, BANK], F32, name="g2_ps%d" % c) for c in range(HALVES)]
 
         y_t = {}
@@ -159,7 +162,18 @@ def tile_transformerblock_pb_t_kernel(tc, y_act, h, W2_words, W2_scales, b2, g2,
         def add_bias(i):
             q, j = divmod(i, PAIR)
             hb[i] = work.tile([P, E], F32, name="hb")
-            nc.gpsimd.tensor_tensor(out=hb[i][:], in0=h_sb[q][:, j, :], in1=b2_all[:], op=ALU.add)
+            nc.gpsimd.tensor_tensor(
+                out=hb[i][:, 0:BIAS_ON_GPSIMD],
+                in0=h_sb[q][:, j, 0:BIAS_ON_GPSIMD],
+                in1=b2_head[:],
+                op=ALU.add,
+            )
+            nc.vector.tensor_tensor(
+                out=hb[i][:, BIAS_ON_GPSIMD:E],
+                in0=h_sb[q][:, j, BIAS_ON_GPSIMD:E],
+                in1=b2_tail[:],
+                op=ALU.add,
+            )
 
         def add_residual(i):
             r[i] = work.tile([P, E], F32, name="r")
@@ -252,6 +266,7 @@ def tile_transformerblock_pb_t_kernel(tc, y_act, h, W2_words, W2_scales, b2, g2,
             for_tile(inverse_std, t - 1)
 
         step(-4)
-        spread_over_partitions(g2_rows, g2_ps)
+        for c in range(HALVES):
+            spread_over_partitions(g2_rows, c * BANK, g2_ps[c])
         for t in range(-3, N_TILES + 2):
             step(t)

@@ -22,9 +22,7 @@ HALVES = E // BANK
 PAIR = 2
 N_TILES = TOKENS // P
 N_PAIRS = N_TILES // PAIR
-PREFETCH = 2
-BIAS_ON_GPSIMD = 768
-BIAS_ON_VECTOR = E - BIAS_ON_GPSIMD
+PREFETCH = 3
 EPS = 1e-5
 
 FLOPS = 2 * TOKENS * K * E
@@ -40,13 +38,12 @@ def tile_transformerblock_pb_t_kernel(tc, y_act, h, W2_words, W2_scales, b2, g2,
     with ExitStack() as ctx:
         ctx.enter_context(tc.manual_schedule())
         const = ctx.enter_context(tc.tile_pool(name="const", bufs=1))
-        loads = ctx.enter_context(tc.tile_pool(name="loads", bufs=4))
+        loads = ctx.enter_context(tc.tile_pool(name="loads", bufs=5))
         quant = ctx.enter_context(tc.tile_pool(name="quant", bufs=2))
-        work = ctx.enter_context(tc.tile_pool(name="work", bufs=4))
-        stats = ctx.enter_context(tc.tile_pool(name="stats", bufs=4))
+        work = ctx.enter_context(tc.tile_pool(name="work", bufs=6))
+        stats = ctx.enter_context(tc.tile_pool(name="stats", bufs=6))
         psum_g2 = ctx.enter_context(tc.psum_pool(name="psum_g2", bufs=1))
-        psum_b2 = ctx.enter_context(tc.psum_pool(name="psum_b2", bufs=1))
-        psum_yt = ctx.enter_context(tc.psum_pool(name="psum_yt", bufs=1))
+        psum_yt = ctx.enter_context(tc.psum_pool(name="psum_yt", bufs=2))
         psum_mm = ctx.enter_context(tc.psum_pool(name="psum_mm", bufs=2))
 
         b2_rows = const.tile([P, E], BF16)
@@ -57,7 +54,7 @@ def tile_transformerblock_pb_t_kernel(tc, y_act, h, W2_words, W2_scales, b2, g2,
         eps = const.tile([P, 1], F32)
         table_warm = const.tile([P, 1], F32)
         ident = const.tile([P, P], F32)
-        b2_head = const.tile([P, BIAS_ON_GPSIMD], F32)
+        b2_all = const.tile([P, E], F32)
 
         nc.vector.memset(b2_rows[:].bitcast(I32), 0)
         nc.vector.memset(w_scales[:].bitcast(I32), 0)
@@ -89,20 +86,20 @@ def tile_transformerblock_pb_t_kernel(tc, y_act, h, W2_words, W2_scales, b2, g2,
         for q in range(1, PREFETCH):
             load_pair(q)
 
-        def spread_over_partitions(rows, first, bank):
-            width = bank.shape[1]
-            nc.tensor.matmul(
-                out=bank[:], lhsT=ones[:], rhs=rows[:, first : first + width], start=True, stop=True
-            )
+        def spread_over_partitions(rows, banks):
+            for c in range(HALVES):
+                nc.tensor.matmul(
+                    out=banks[c][:],
+                    lhsT=ones[:],
+                    rhs=rows[:, c * BANK : (c + 1) * BANK],
+                    start=True,
+                    stop=True,
+                )
 
-        b2_ps0 = psum_mm.tile([P, BANK], F32, name="mm0")
-        b2_ps1 = psum_mm.tile([P, BIAS_ON_GPSIMD - BANK], F32, name="mm1")
-        b2_tail = psum_b2.tile([P, BIAS_ON_VECTOR], F32)
-        spread_over_partitions(b2_rows, 0, b2_ps0)
-        spread_over_partitions(b2_rows, BANK, b2_ps1)
-        spread_over_partitions(b2_rows, BIAS_ON_GPSIMD, b2_tail)
-        nc.scalar.copy(out=b2_head[:, 0:BANK], in_=b2_ps0[:])
-        nc.vector.tensor_copy(out=b2_head[:, BANK:BIAS_ON_GPSIMD], in_=b2_ps1[:])
+        b2_ps = [psum_mm.tile([P, BANK], F32, name="mm%d" % c) for c in range(HALVES)]
+        spread_over_partitions(b2_rows, b2_ps)
+        nc.scalar.copy(out=b2_all[:, 0:BANK], in_=b2_ps[0][:])
+        nc.vector.tensor_copy(out=b2_all[:, BANK:E], in_=b2_ps[1][:])
         g2_ps = [psum_g2.tile([P, BANK], F32, name="g2_ps%d" % c) for c in range(HALVES)]
 
         y_t = {}
@@ -162,18 +159,7 @@ def tile_transformerblock_pb_t_kernel(tc, y_act, h, W2_words, W2_scales, b2, g2,
         def add_bias(i):
             q, j = divmod(i, PAIR)
             hb[i] = work.tile([P, E], F32, name="hb")
-            nc.gpsimd.tensor_tensor(
-                out=hb[i][:, 0:BIAS_ON_GPSIMD],
-                in0=h_sb[q][:, j, 0:BIAS_ON_GPSIMD],
-                in1=b2_head[:],
-                op=ALU.add,
-            )
-            nc.vector.tensor_tensor(
-                out=hb[i][:, BIAS_ON_GPSIMD:E],
-                in0=h_sb[q][:, j, BIAS_ON_GPSIMD:E],
-                in1=b2_tail[:],
-                op=ALU.add,
-            )
+            nc.gpsimd.tensor_tensor(out=hb[i][:], in0=h_sb[q][:, j, :], in1=b2_all[:], op=ALU.add)
 
         def add_residual(i):
             r[i] = work.tile([P, E], F32, name="r")
@@ -253,20 +239,19 @@ def tile_transformerblock_pb_t_kernel(tc, y_act, h, W2_words, W2_scales, b2, g2,
 
         def step(t):
             for_pair(load_pair, t + 4 + PAIR * PREFETCH)
-            for_pair(transpose_pair, t + 4)
-            for_pair(group_pair, t + 3)
-            for_pair(quantise_pair, t + 2)
+            for_pair(transpose_pair, t + 5)
+            for_pair(group_pair, t + 4)
             for_tile(add_bias, t + 2)
             for_tile(multiply, t + 1)
             for_tile(add_residual, t)
+            for_pair(quantise_pair, t + 3)
             for_tile(centre_and_gain, t - 1)
             for_tile(mean, t)
             for_tile(squares, t - 1)
             for_tile(scale_and_store, t - 2)
             for_tile(inverse_std, t - 1)
 
-        step(-4)
-        for c in range(HALVES):
-            spread_over_partitions(g2_rows, c * BANK, g2_ps[c])
-        for t in range(-3, N_TILES + 2):
+        step(-5)
+        spread_over_partitions(g2_rows, g2_ps)
+        for t in range(-4, N_TILES + 2):
             step(t)

@@ -23,6 +23,7 @@ PAIR = 2
 N_TILES = TOKENS // P
 N_PAIRS = N_TILES // PAIR
 PREFETCH = 3
+BIAS_ON_GPSIMD = 896
 EPS = 1e-5
 
 FLOPS = 2 * TOKENS * K * E
@@ -43,7 +44,8 @@ def tile_transformerblock_pb_t_kernel(tc, y_act, h, W2_words, W2_scales, b2, g2,
         work = ctx.enter_context(tc.tile_pool(name="work", bufs=6))
         stats = ctx.enter_context(tc.tile_pool(name="stats", bufs=6))
         psum_g2 = ctx.enter_context(tc.psum_pool(name="psum_g2", bufs=1))
-        psum_yt = ctx.enter_context(tc.psum_pool(name="psum_yt", bufs=2))
+        psum_b2 = ctx.enter_context(tc.psum_pool(name="psum_b2", bufs=1))
+        psum_yt = ctx.enter_context(tc.psum_pool(name="psum_yt", bufs=1))
         psum_mm = ctx.enter_context(tc.psum_pool(name="psum_mm", bufs=2))
 
         b2_rows = const.tile([P, E], BF16)
@@ -54,7 +56,7 @@ def tile_transformerblock_pb_t_kernel(tc, y_act, h, W2_words, W2_scales, b2, g2,
         eps = const.tile([P, 1], F32)
         table_warm = const.tile([P, 1], F32)
         ident = const.tile([P, P], F32)
-        b2_all = const.tile([P, E], F32)
+        b2_sb = const.tile([P, BIAS_ON_GPSIMD], F32)
 
         nc.vector.memset(b2_rows[:].bitcast(I32), 0)
         nc.vector.memset(w_scales[:].bitcast(I32), 0)
@@ -96,10 +98,13 @@ def tile_transformerblock_pb_t_kernel(tc, y_act, h, W2_words, W2_scales, b2, g2,
                     stop=True,
                 )
 
-        b2_ps = [psum_mm.tile([P, BANK], F32, name="mm%d" % c) for c in range(HALVES)]
+        b2_ps = [
+            psum_mm.tile([P, BANK], F32, name="mm0"),
+            psum_b2.tile([P, BANK], F32, name="b2_upper"),
+        ]
         spread_over_partitions(b2_rows, b2_ps)
-        nc.scalar.copy(out=b2_all[:, 0:BANK], in_=b2_ps[0][:])
-        nc.vector.tensor_copy(out=b2_all[:, BANK:E], in_=b2_ps[1][:])
+        nc.scalar.copy(out=b2_sb[:, 0:BANK], in_=b2_ps[0][:])
+        nc.vector.tensor_copy(out=b2_sb[:, BANK:BIAS_ON_GPSIMD], in_=b2_ps[1][:, 0 : BIAS_ON_GPSIMD - BANK])
         g2_ps = [psum_g2.tile([P, BANK], F32, name="g2_ps%d" % c) for c in range(HALVES)]
 
         y_t = {}
@@ -159,7 +164,18 @@ def tile_transformerblock_pb_t_kernel(tc, y_act, h, W2_words, W2_scales, b2, g2,
         def add_bias(i):
             q, j = divmod(i, PAIR)
             hb[i] = work.tile([P, E], F32, name="hb")
-            nc.gpsimd.tensor_tensor(out=hb[i][:], in0=h_sb[q][:, j, :], in1=b2_all[:], op=ALU.add)
+            nc.gpsimd.tensor_tensor(
+                out=hb[i][:, 0:BIAS_ON_GPSIMD],
+                in0=h_sb[q][:, j, 0:BIAS_ON_GPSIMD],
+                in1=b2_sb[:],
+                op=ALU.add,
+            )
+            nc.vector.tensor_tensor(
+                out=hb[i][:, BIAS_ON_GPSIMD:E],
+                in0=h_sb[q][:, j, BIAS_ON_GPSIMD:E],
+                in1=b2_ps[1][:, BIAS_ON_GPSIMD - BANK : BANK],
+                op=ALU.add,
+            )
 
         def add_residual(i):
             r[i] = work.tile([P, E], F32, name="r")

@@ -21,10 +21,25 @@ BANK = 512
 HALVES = E // BANK
 PAIR = 2
 N_TILES = TOKENS // P
-N_PAIRS = N_TILES // PAIR
-PREFETCH = 3
-BIAS_ON_GPSIMD = 896
 EPS = 1e-5
+
+BIAS_ON_GPSIMD = 960
+
+LOAD_LEAD = 10
+TRANSPOSE_LEAD = 4
+GROUP_LEAD = 3
+QUANTISE_LEAD = 2
+BIAS_LEAD = 2
+MULTIPLY_LEAD = 1
+GAIN_LAG = 1
+SQUARES_LAG = 1
+SCALE_LAG = 2
+FIRST_STEP = -TRANSPOSE_LEAD
+LAST_STEP = N_TILES - 1 + SCALE_LAG
+
+LOAD_BUFS = LOAD_LEAD // PAIR
+QUANT_BUFS = 2
+WORK_BUFS = 6
 
 FLOPS = 2 * TOKENS * K * E
 
@@ -39,10 +54,10 @@ def tile_transformerblock_pb_t_kernel(tc, y_act, h, W2_words, W2_scales, b2, g2,
     with ExitStack() as ctx:
         ctx.enter_context(tc.manual_schedule())
         const = ctx.enter_context(tc.tile_pool(name="const", bufs=1))
-        loads = ctx.enter_context(tc.tile_pool(name="loads", bufs=5))
-        quant = ctx.enter_context(tc.tile_pool(name="quant", bufs=2))
-        work = ctx.enter_context(tc.tile_pool(name="work", bufs=6))
-        stats = ctx.enter_context(tc.tile_pool(name="stats", bufs=6))
+        loads = ctx.enter_context(tc.tile_pool(name="loads", bufs=LOAD_BUFS))
+        quant = ctx.enter_context(tc.tile_pool(name="quant", bufs=QUANT_BUFS))
+        work = ctx.enter_context(tc.tile_pool(name="work", bufs=WORK_BUFS))
+        stats = ctx.enter_context(tc.tile_pool(name="stats", bufs=WORK_BUFS))
         psum_g2 = ctx.enter_context(tc.psum_pool(name="psum_g2", bufs=1))
         psum_b2 = ctx.enter_context(tc.psum_pool(name="psum_b2", bufs=1))
         psum_yt = ctx.enter_context(tc.psum_pool(name="psum_yt", bufs=1))
@@ -85,7 +100,7 @@ def tile_transformerblock_pb_t_kernel(tc, y_act, h, W2_words, W2_scales, b2, g2,
                 out=w_scales[32 * quadrant : 32 * quadrant + 4, :].bitcast(I32),
                 in_=W2_scales[0, 4 * quadrant : 4 * quadrant + 4, :].bitcast(I32),
             )
-        for q in range(1, PREFETCH):
+        for q in range(1, (LOAD_LEAD + FIRST_STEP) // PAIR):
             load_pair(q)
 
         def spread_over_partitions(rows, banks):
@@ -98,13 +113,13 @@ def tile_transformerblock_pb_t_kernel(tc, y_act, h, W2_words, W2_scales, b2, g2,
                     stop=True,
                 )
 
-        b2_ps = [
-            psum_mm.tile([P, BANK], F32, name="mm0"),
-            psum_b2.tile([P, BANK], F32, name="b2_upper"),
-        ]
-        spread_over_partitions(b2_rows, b2_ps)
-        nc.scalar.copy(out=b2_sb[:, 0:BANK], in_=b2_ps[0][:])
-        nc.vector.tensor_copy(out=b2_sb[:, BANK:BIAS_ON_GPSIMD], in_=b2_ps[1][:, 0 : BIAS_ON_GPSIMD - BANK])
+        b2_lower = psum_mm.tile([P, BANK], F32, name="mm0")
+        b2_upper = psum_b2.tile([P, BANK], F32)
+        spread_over_partitions(b2_rows, [b2_lower, b2_upper])
+        nc.scalar.copy(out=b2_sb[:, 0:BANK], in_=b2_lower[:])
+        nc.vector.tensor_copy(
+            out=b2_sb[:, BANK:BIAS_ON_GPSIMD], in_=b2_upper[:, 0 : BIAS_ON_GPSIMD - BANK]
+        )
         g2_ps = [psum_g2.tile([P, BANK], F32, name="g2_ps%d" % c) for c in range(HALVES)]
 
         y_t = {}
@@ -173,7 +188,7 @@ def tile_transformerblock_pb_t_kernel(tc, y_act, h, W2_words, W2_scales, b2, g2,
             nc.vector.tensor_tensor(
                 out=hb[i][:, BIAS_ON_GPSIMD:E],
                 in0=h_sb[q][:, j, BIAS_ON_GPSIMD:E],
-                in1=b2_ps[1][:, BIAS_ON_GPSIMD - BANK : BANK],
+                in1=b2_upper[:, BIAS_ON_GPSIMD - BANK : BANK],
                 op=ALU.add,
             )
 
@@ -254,20 +269,20 @@ def tile_transformerblock_pb_t_kernel(tc, y_act, h, W2_words, W2_scales, b2, g2,
                 stage(first_tile // PAIR)
 
         def step(t):
-            for_pair(load_pair, t + 4 + PAIR * PREFETCH)
-            for_pair(transpose_pair, t + 5)
-            for_pair(group_pair, t + 4)
-            for_tile(add_bias, t + 2)
-            for_tile(multiply, t + 1)
+            for_pair(load_pair, t + LOAD_LEAD)
+            for_pair(transpose_pair, t + TRANSPOSE_LEAD)
+            for_pair(group_pair, t + GROUP_LEAD)
+            for_tile(add_bias, t + BIAS_LEAD)
+            for_tile(multiply, t + MULTIPLY_LEAD)
             for_tile(add_residual, t)
-            for_pair(quantise_pair, t + 3)
-            for_tile(centre_and_gain, t - 1)
+            for_pair(quantise_pair, t + QUANTISE_LEAD)
+            for_tile(centre_and_gain, t - GAIN_LAG)
             for_tile(mean, t)
-            for_tile(squares, t - 1)
-            for_tile(scale_and_store, t - 2)
-            for_tile(inverse_std, t - 1)
+            for_tile(squares, t - SQUARES_LAG)
+            for_tile(scale_and_store, t - SCALE_LAG)
+            for_tile(inverse_std, t - SQUARES_LAG)
 
-        step(-5)
+        step(FIRST_STEP)
         spread_over_partitions(g2_rows, g2_ps)
-        for t in range(-4, N_TILES + 2):
+        for t in range(FIRST_STEP + 1, LAST_STEP + 1):
             step(t)

@@ -106,7 +106,7 @@ def tile_transformerblock_pb_t_kernel(tc, y_act, h, W2_words, W2_scales, b2, g2,
         def spread_over_partitions(rows, banks):
             for c in range(HALVES):
                 nc.tensor.matmul(
-                    out=banks[c][:],
+                    out=banks[c],
                     lhsT=ones[:],
                     rhs=rows[:, c * BANK : (c + 1) * BANK],
                     start=True,
@@ -115,12 +115,12 @@ def tile_transformerblock_pb_t_kernel(tc, y_act, h, W2_words, W2_scales, b2, g2,
 
         b2_lower = psum_mm.tile([P, BANK], F32, name="mm0")
         b2_upper = psum_b2.tile([P, BANK], F32)
-        spread_over_partitions(b2_rows, [b2_lower, b2_upper])
+        spread_over_partitions(b2_rows, [b2_lower[:], b2_upper[:]])
         nc.scalar.copy(out=b2_sb[:, 0:BANK], in_=b2_lower[:])
         nc.vector.tensor_copy(
             out=b2_sb[:, BANK:BIAS_ON_GPSIMD], in_=b2_upper[:, 0 : BIAS_ON_GPSIMD - BANK]
         )
-        g2_ps = [psum_g2.tile([P, BANK], F32, name="g2_ps%d" % c) for c in range(HALVES)]
+        g2_ps = psum_g2.tile([P, E], BF16, name="g2_ps")
 
         y_t = {}
         grouped = {}
@@ -234,16 +234,14 @@ def tile_transformerblock_pb_t_kernel(tc, y_act, h, W2_words, W2_scales, b2, g2,
 
         def centre_and_gain(i):
             z[i] = work.tile([P, E], F32, name="z")
-            for c in range(HALVES):
-                cols = slice(c * BANK, (c + 1) * BANK)
-                nc.vector.scalar_tensor_tensor(
-                    out=z[i][:, cols],
-                    in0=r[i][:, cols],
-                    scalar=neg_mean[i][:, 0:1],
-                    in1=g2_ps[c][:],
-                    op0=ALU.add,
-                    op1=ALU.mult,
-                )
+            nc.vector.scalar_tensor_tensor(
+                out=z[i][:],
+                in0=r[i][:],
+                scalar=neg_mean[i][:, 0:1],
+                in1=g2_ps[:],
+                op0=ALU.add,
+                op1=ALU.mult,
+            )
 
         def inverse_std(i):
             rstd[i] = stats.tile([P, 1], F32, name="rstd")
@@ -283,6 +281,6 @@ def tile_transformerblock_pb_t_kernel(tc, y_act, h, W2_words, W2_scales, b2, g2,
             for_tile(inverse_std, t - SQUARES_LAG)
 
         step(FIRST_STEP)
-        spread_over_partitions(g2_rows, g2_ps)
+        spread_over_partitions(g2_rows, [g2_ps[:, c * BANK : (c + 1) * BANK] for c in range(HALVES)])
         for t in range(FIRST_STEP + 1, LAST_STEP + 1):
             step(t)

@@ -210,13 +210,11 @@ def tile_transformerblock_pb_t_kernel(tc, y_act, h, W2_words, W2_scales, b2, g2,
         def mean(i):
             scaled_sums = stats.tile([P, HALVES], F32, name="scaled_sums")
             neg_mean[i] = stats.tile([P, 1], F32, name="neg_mean")
-            nc.vector.tensor_scalar(
+            nc.scalar.activation(
                 out=scaled_sums[:],
-                in0=sums[i][:],
-                scalar1=-1.0 / E,
-                scalar2=None,
-                op0=ALU.mult,
-                op1=ALU.add,
+                in_=sums[i][:],
+                func=ACT.Copy,
+                scale=-1.0 / E,
                 accum_out=neg_mean[i][:],
             )
 
@@ -275,10 +273,10 @@ def tile_transformerblock_pb_t_kernel(tc, y_act, h, W2_words, W2_scales, b2, g2,
             for_tile(add_residual, t)
             for_pair(quantise_pair, t + QUANTISE_LEAD)
             for_tile(centre_and_gain, t - GAIN_LAG)
-            for_tile(mean, t)
             for_tile(squares, t - SQUARES_LAG)
             for_tile(scale_and_store, t - SCALE_LAG)
             for_tile(inverse_std, t - SQUARES_LAG)
+            for_tile(mean, t)
 
         step(FIRST_STEP)
         spread_over_partitions(g2_rows, [g2_ps[:, c * BANK : (c + 1) * BANK] for c in range(HALVES)])

@@ -23,7 +23,7 @@ PAIR = 2
 N_TILES = TOKENS // P
 EPS = 1e-5
 
-BIAS_ON_GPSIMD = 960
+BIAS_ON_GPSIMD = 880
 
 LOAD_LEAD = 10
 TRANSPOSE_LEAD = 4

@@ -40,6 +40,7 @@ LAST_STEP = N_TILES - 1 + SCALE_LAG
 LOAD_BUFS = LOAD_LEAD // PAIR
 QUANT_BUFS = 2
 WORK_BUFS = 6
+BIAS_BUFS = 3
 
 FLOPS = 2 * TOKENS * K * E
 
@@ -58,6 +59,7 @@ def tile_transformerblock_pb_t_kernel(tc, y_act, h, W2_words, W2_scales, b2, g2,
         quant = ctx.enter_context(tc.tile_pool(name="quant", bufs=QUANT_BUFS))
         work = ctx.enter_context(tc.tile_pool(name="work", bufs=WORK_BUFS))
         stats = ctx.enter_context(tc.tile_pool(name="stats", bufs=WORK_BUFS))
+        biased = ctx.enter_context(tc.tile_pool(name="biased", bufs=BIAS_BUFS))
         psum_g2 = ctx.enter_context(tc.psum_pool(name="psum_g2", bufs=1))
         psum_b2 = ctx.enter_context(tc.psum_pool(name="psum_b2", bufs=1))
         psum_yt = ctx.enter_context(tc.psum_pool(name="psum_yt", bufs=1))
@@ -178,7 +180,7 @@ def tile_transformerblock_pb_t_kernel(tc, y_act, h, W2_words, W2_scales, b2, g2,
 
         def add_bias(i):
             q, j = divmod(i, PAIR)
-            hb[i] = work.tile([P, E], F32, name="hb")
+            hb[i] = biased.tile([P, E], F32, name="hb")
             nc.gpsimd.tensor_tensor(
                 out=hb[i][:, 0:BIAS_ON_GPSIMD],
                 in0=h_sb[q][:, j, 0:BIAS_ON_GPSIMD],

@@ -29,7 +29,7 @@ LOAD_LEAD = 10
 TRANSPOSE_LEAD = 4
 GROUP_LEAD = 3
 QUANTISE_LEAD = 2
-BIAS_LEAD = 2
+BIAS_LEADS = (3, 4)
 MULTIPLY_LEAD = 1
 GAIN_LAG = 1
 SQUARES_LAG = 1
@@ -40,7 +40,7 @@ LAST_STEP = N_TILES - 1 + SCALE_LAG
 LOAD_BUFS = LOAD_LEAD // PAIR
 QUANT_BUFS = 2
 WORK_BUFS = 6
-BIAS_BUFS = 3
+BIAS_BUFS = 2
 
 FLOPS = 2 * TOKENS * K * E
 
@@ -180,7 +180,10 @@ def tile_transformerblock_pb_t_kernel(tc, y_act, h, W2_words, W2_scales, b2, g2,
 
         def add_bias(i):
             q, j = divmod(i, PAIR)
-            hb[i] = biased.tile([P, E], F32, name="hb")
+            if i % PAIR == 1 or i == 0:
+                two_tiles = biased.tile([P, PAIR, E], F32, name="hb")
+                hb[i] = two_tiles[:, 0, :]
+                hb[i + 1] = two_tiles[:, 1, :]
             nc.gpsimd.tensor_tensor(
                 out=hb[i][:, 0:BIAS_ON_GPSIMD],
                 in0=h_sb[q][:, j, 0:BIAS_ON_GPSIMD],
@@ -270,10 +273,12 @@ def tile_transformerblock_pb_t_kernel(tc, y_act, h, W2_words, W2_scales, b2, g2,
             for_pair(load_pair, t + LOAD_LEAD)
             for_pair(transpose_pair, t + TRANSPOSE_LEAD)
             for_pair(group_pair, t + GROUP_LEAD)
-            for_tile(add_bias, t + BIAS_LEAD)
             for_tile(multiply, t + MULTIPLY_LEAD)
             for_tile(add_residual, t)
             for_pair(quantise_pair, t + QUANTISE_LEAD)
+            if t % PAIR == 0:
+                for lead in BIAS_LEADS:
+                    for_tile(add_bias, t + lead)
             for_tile(centre_and_gain, t - GAIN_LAG)
             for_tile(squares, t - SQUARES_LAG)
             for_tile(scale_and_store, t - SCALE_LAG)

@@ -21,9 +21,10 @@ BANK = 512
 HALVES = E // BANK
 PAIR = 2
 N_TILES = TOKENS // P
+LAST_TILE = N_TILES - 1
 EPS = 1e-5
 
-BIAS_ON_GPSIMD = 880
+BIAS_ON_GPSIMD = 912
 
 LOAD_LEAD = 10
 TRANSPOSE_LEAD = 4
@@ -75,8 +76,8 @@ def tile_transformerblock_pb_t_kernel(tc, y_act, h, W2_words, W2_scales, b2, g2,
         ident = const.tile([P, P], F32)
         b2_sb = const.tile([P, BIAS_ON_GPSIMD], F32)
 
-        nc.vector.memset(b2_rows[:].bitcast(I32), 0)
         nc.vector.memset(w_scales[:].bitcast(I32), 0)
+        nc.vector.memset(b2_rows[:].bitcast(I32), 0)
         nc.vector.memset(g2_rows[:].bitcast(I32), 0)
         nc.vector.memset(ones[:], 1.0)
         nc.vector.memset(eps[:], EPS)
@@ -89,19 +90,26 @@ def tile_transformerblock_pb_t_kernel(tc, y_act, h, W2_words, W2_scales, b2, g2,
         y_sb = {}
         h_sb = {}
 
-        def load_pair(q):
+        def load_y(q):
             y_sb[q] = loads.tile([P, PAIR, K], BF16, name="y_sb")
             nc.sync.dma_start(out=y_sb[q][:], in_=y_pairs[q])
+
+        def load_h(q):
             h_sb[q] = loads.tile([P, PAIR, E], BF16, name="h_sb")
             nc.sync.dma_start(out=h_sb[q][:], in_=h_pairs[q])
 
-        load_pair(0)
-        nc.sync.dma_start(out=w_words[:].bitcast(I32), in_=W2_words[0].bitcast(I32))
+        def load_pair(q):
+            load_y(q)
+            load_h(q)
+
+        load_y(0)
         for quadrant in range(4):
             nc.sync.dma_start(
                 out=w_scales[32 * quadrant : 32 * quadrant + 4, :].bitcast(I32),
                 in_=W2_scales[0, 4 * quadrant : 4 * quadrant + 4, :].bitcast(I32),
             )
+        nc.sync.dma_start(out=w_words[:].bitcast(I32), in_=W2_words[0].bitcast(I32))
+        load_h(0)
         for q in range(1, (LOAD_LEAD + FIRST_STEP) // PAIR):
             load_pair(q)
 
@@ -235,16 +243,22 @@ def tile_transformerblock_pb_t_kernel(tc, y_act, h, W2_words, W2_scales, b2, g2,
                 accum_out=ssq[i][:],
             )
 
+        def pieces_of(i):
+            if i == LAST_TILE:
+                return [slice(c * BANK, (c + 1) * BANK) for c in range(HALVES)]
+            return [slice(0, E)]
+
         def centre_and_gain(i):
             z[i] = work.tile([P, E], F32, name="z")
-            nc.vector.scalar_tensor_tensor(
-                out=z[i][:],
-                in0=r[i][:],
-                scalar=neg_mean[i][:, 0:1],
-                in1=g2_ps[:],
-                op0=ALU.add,
-                op1=ALU.mult,
-            )
+            for cols in pieces_of(i):
+                nc.vector.scalar_tensor_tensor(
+                    out=z[i][:, cols],
+                    in0=r[i][:, cols],
+                    scalar=neg_mean[i][:, 0:1],
+                    in1=g2_ps[:, cols],
+                    op0=ALU.add,
+                    op1=ALU.mult,
+                )
 
         def inverse_std(i):
             rstd[i] = stats.tile([P, 1], F32, name="rstd")
@@ -258,8 +272,22 @@ def tile_transformerblock_pb_t_kernel(tc, y_act, h, W2_words, W2_scales, b2, g2,
 
         def scale_and_store(i):
             q, j = divmod(i, PAIR)
-            nc.scalar.activation(out=z[i][:], in_=z[i][:], func=ACT.Copy, scale=rstd[i][:, 0:1])
-            nc.sync.dma_start(out=out_pairs[q][:, j, :], in_=z[i][:])
+            if i == LAST_TILE - 1:
+                nc.gpsimd.tensor_scalar(
+                    out=z[i][:],
+                    in0=z[i][:],
+                    scalar1=rstd[i][:, 0:1],
+                    scalar2=0.0,
+                    op0=ALU.mult,
+                    op1=ALU.add,
+                )
+                nc.sync.dma_start(out=out_pairs[q][:, j, :], in_=z[i][:])
+                return
+            for cols in pieces_of(i):
+                nc.scalar.activation(
+                    out=z[i][:, cols], in_=z[i][:, cols], func=ACT.Copy, scale=rstd[i][:, 0:1]
+                )
+                nc.sync.dma_start(out=out_pairs[q][:, j, cols], in_=z[i][:, cols])
 
         def for_tile(stage, i):
             if 0 <= i < N_TILES:

@@ -22,6 +22,7 @@ HALVES = E // BANK
 PAIR = 2
 N_TILES = TOKENS // P
 LAST_TILE = N_TILES - 1
+SCALED_BY_GPSIMD = range(LAST_TILE - 4, LAST_TILE)
 EPS = 1e-5
 
 BIAS_ON_GPSIMD = 912
@@ -272,7 +273,7 @@ def tile_transformerblock_pb_t_kernel(tc, y_act, h, W2_words, W2_scales, b2, g2,
 
         def scale_and_store(i):
             q, j = divmod(i, PAIR)
-            if i == LAST_TILE - 1:
+            if i in SCALED_BY_GPSIMD:
                 nc.gpsimd.tensor_scalar(
                     out=z[i][:],
                     in0=z[i][:],

@@ -26,6 +26,7 @@ SCALED_BY_GPSIMD = range(LAST_TILE - 4, LAST_TILE)
 EPS = 1e-5
 
 BIAS_ON_GPSIMD = 912
+BIASED_BY_VECTOR = 2
 
 LOAD_LEAD = 10
 TRANSPOSE_LEAD = 4
@@ -77,16 +78,16 @@ def tile_transformerblock_pb_t_kernel(tc, y_act, h, W2_words, W2_scales, b2, g2,
         ident = const.tile([P, P], F32)
         b2_sb = const.tile([P, BIAS_ON_GPSIMD], F32)
 
-        nc.vector.memset(w_scales[:].bitcast(I32), 0)
         nc.vector.memset(b2_rows[:].bitcast(I32), 0)
-        nc.vector.memset(g2_rows[:].bitcast(I32), 0)
-        nc.vector.memset(ones[:], 1.0)
+        nc.vector.memset(w_scales[:].bitcast(I32), 0)
         nc.vector.memset(eps[:], EPS)
+        nc.vector.memset(ones[:], 1.0)
+        nc.vector.memset(g2_rows[:].bitcast(I32), 0)
         make_identity(nc, ident[:])
 
         nc.scalar.dma_start(out=b2_rows[0:1, :], in_=b2.unsqueeze(0))
-        nc.scalar.dma_start(out=g2_rows[0:1, :], in_=g2.unsqueeze(0))
         nc.scalar.activation(out=table_warm[:], in_=eps[:], func=ACT.Abs_reciprocal_sqrt)
+        nc.scalar.dma_start(out=g2_rows[0:1, :], in_=g2.unsqueeze(0))
 
         y_sb = {}
         h_sb = {}
@@ -110,7 +111,9 @@ def tile_transformerblock_pb_t_kernel(tc, y_act, h, W2_words, W2_scales, b2, g2,
                 in_=W2_scales[0, 4 * quadrant : 4 * quadrant + 4, :].bitcast(I32),
             )
         nc.sync.dma_start(out=w_words[:].bitcast(I32), in_=W2_words[0].bitcast(I32))
-        load_h(0)
+        h_sb[0] = loads.tile([P, PAIR, E], BF16, name="h_sb")
+        for j in range(PAIR):
+            nc.sync.dma_start(out=h_sb[0][:, j, :], in_=h_pairs[0][:, j, :])
         for q in range(1, (LOAD_LEAD + FIRST_STEP) // PAIR):
             load_pair(q)
 
@@ -128,9 +131,6 @@ def tile_transformerblock_pb_t_kernel(tc, y_act, h, W2_words, W2_scales, b2, g2,
         b2_upper = psum_b2.tile([P, BANK], F32)
         spread_over_partitions(b2_rows, [b2_lower[:], b2_upper[:]])
         nc.scalar.copy(out=b2_sb[:, 0:BANK], in_=b2_lower[:])
-        nc.vector.tensor_copy(
-            out=b2_sb[:, BANK:BIAS_ON_GPSIMD], in_=b2_upper[:, 0 : BIAS_ON_GPSIMD - BANK]
-        )
         g2_ps = psum_g2.tile([P, E], BF16, name="g2_ps")
 
         y_t = {}
@@ -193,6 +193,13 @@ def tile_transformerblock_pb_t_kernel(tc, y_act, h, W2_words, W2_scales, b2, g2,
                 two_tiles = biased.tile([P, PAIR, E], F32, name="hb")
                 hb[i] = two_tiles[:, 0, :]
                 hb[i + 1] = two_tiles[:, 1, :]
+            if i < BIASED_BY_VECTOR:
+                for c, b2_bank in enumerate([b2_lower, b2_upper]):
+                    cols = slice(c * BANK, (c + 1) * BANK)
+                    nc.vector.tensor_tensor(
+                        out=hb[i][:, cols], in0=h_sb[q][:, j, cols], in1=b2_bank[:], op=ALU.add
+                    )
+                return
             nc.gpsimd.tensor_tensor(
                 out=hb[i][:, 0:BIAS_ON_GPSIMD],
                 in0=h_sb[q][:, j, 0:BIAS_ON_GPSIMD],
@@ -316,5 +323,9 @@ def tile_transformerblock_pb_t_kernel(tc, y_act, h, W2_words, W2_scales, b2, g2,
 
         step(FIRST_STEP)
         spread_over_partitions(g2_rows, [g2_ps[:, c * BANK : (c + 1) * BANK] for c in range(HALVES)])
-        for t in range(FIRST_STEP + 1, LAST_STEP + 1):
+        step(FIRST_STEP + 1)
+        nc.scalar.copy(
+            out=b2_sb[:, BANK:BIAS_ON_GPSIMD], in_=b2_upper[:, 0 : BIAS_ON_GPSIMD - BANK]
+        )
+        for t in range(FIRST_STEP + 2, LAST_STEP + 1):
             step(t)

@@ -25,7 +25,7 @@ LAST_TILE = N_TILES - 1
 SCALED_BY_GPSIMD = range(LAST_TILE - 4, LAST_TILE)
 EPS = 1e-5
 
-BIAS_ON_GPSIMD = 912
+BIAS_ON_GPSIMD = 960
 BIASED_BY_VECTOR = 2
 
 LOAD_LEAD = 10

@@ -25,14 +25,14 @@ LAST_TILE = N_TILES - 1
 SCALED_BY_GPSIMD = range(LAST_TILE - 4, LAST_TILE)
 EPS = 1e-5
 
-BIAS_ON_GPSIMD = 960
+N_COUPLES = N_TILES // PAIR + 1
 BIASED_BY_VECTOR = 2
 
 LOAD_LEAD = 10
 TRANSPOSE_LEAD = 4
 GROUP_LEAD = 3
 QUANTISE_LEAD = 2
-BIAS_LEADS = (3, 4)
+BIAS_LEAD = 4
 MULTIPLY_LEAD = 1
 GAIN_LAG = 1
 SQUARES_LAG = 1
@@ -76,7 +76,7 @@ def tile_transformerblock_pb_t_kernel(tc, y_act, h, W2_words, W2_scales, b2, g2,
         eps = const.tile([P, 1], F32)
         table_warm = const.tile([P, 1], F32)
         ident = const.tile([P, P], F32)
-        b2_sb = const.tile([P, BIAS_ON_GPSIMD], F32)
+        b2_sb = const.tile([P, E], F32)
 
         nc.vector.memset(b2_rows[:].bitcast(I32), 0)
         nc.vector.memset(w_scales[:].bitcast(I32), 0)
@@ -96,13 +96,17 @@ def tile_transformerblock_pb_t_kernel(tc, y_act, h, W2_words, W2_scales, b2, g2,
             y_sb[q] = loads.tile([P, PAIR, K], BF16, name="y_sb")
             nc.sync.dma_start(out=y_sb[q][:], in_=y_pairs[q])
 
-        def load_h(q):
-            h_sb[q] = loads.tile([P, PAIR, E], BF16, name="h_sb")
-            nc.sync.dma_start(out=h_sb[q][:], in_=h_pairs[q])
+        def place_of(i):
+            return divmod(i + 1, PAIR)
 
-        def load_pair(q):
-            load_y(q)
-            load_h(q)
+        def tiles_of(m):
+            return [i for i in (PAIR * m - 1, PAIR * m) if 0 <= i < N_TILES]
+
+        def load_h(m):
+            h_sb[m] = loads.tile([P, PAIR, E], BF16, name="h_sb")
+            for i in tiles_of(m):
+                q, j = divmod(i, PAIR)
+                nc.sync.dma_start(out=h_sb[m][:, place_of(i)[1], :], in_=h_pairs[q][:, j, :])
 
         load_y(0)
         for quadrant in range(4):
@@ -111,11 +115,11 @@ def tile_transformerblock_pb_t_kernel(tc, y_act, h, W2_words, W2_scales, b2, g2,
                 in_=W2_scales[0, 4 * quadrant : 4 * quadrant + 4, :].bitcast(I32),
             )
         nc.sync.dma_start(out=w_words[:].bitcast(I32), in_=W2_words[0].bitcast(I32))
-        h_sb[0] = loads.tile([P, PAIR, E], BF16, name="h_sb")
-        for j in range(PAIR):
-            nc.sync.dma_start(out=h_sb[0][:, j, :], in_=h_pairs[0][:, j, :])
-        for q in range(1, (LOAD_LEAD + FIRST_STEP) // PAIR):
-            load_pair(q)
+        load_h(0)
+        load_h(1)
+        load_y(1)
+        load_y(2)
+        load_h(2)
 
         def spread_over_partitions(rows, banks):
             for c in range(HALVES):
@@ -131,6 +135,7 @@ def tile_transformerblock_pb_t_kernel(tc, y_act, h, W2_words, W2_scales, b2, g2,
         b2_upper = psum_b2.tile([P, BANK], F32)
         spread_over_partitions(b2_rows, [b2_lower[:], b2_upper[:]])
         nc.scalar.copy(out=b2_sb[:, 0:BANK], in_=b2_lower[:])
+        nc.scalar.copy(out=b2_sb[:, BANK:E], in_=b2_upper[:])
         g2_ps = psum_g2.tile([P, E], BF16, name="g2_ps")
 
         y_t = {}
@@ -187,40 +192,38 @@ def tile_transformerblock_pb_t_kernel(tc, y_act, h, W2_words, W2_scales, b2, g2,
                     stop=True,
                 )
 
-        def add_bias(i):
-            q, j = divmod(i, PAIR)
-            if i % PAIR == 1 or i == 0:
-                two_tiles = biased.tile([P, PAIR, E], F32, name="hb")
-                hb[i] = two_tiles[:, 0, :]
-                hb[i + 1] = two_tiles[:, 1, :]
-            if i < BIASED_BY_VECTOR:
-                for c, b2_bank in enumerate([b2_lower, b2_upper]):
-                    cols = slice(c * BANK, (c + 1) * BANK)
-                    nc.vector.tensor_tensor(
-                        out=hb[i][:, cols], in0=h_sb[q][:, j, cols], in1=b2_bank[:], op=ALU.add
-                    )
-                return
-            nc.gpsimd.tensor_tensor(
-                out=hb[i][:, 0:BIAS_ON_GPSIMD],
-                in0=h_sb[q][:, j, 0:BIAS_ON_GPSIMD],
-                in1=b2_sb[:],
-                op=ALU.add,
-            )
-            nc.vector.tensor_tensor(
-                out=hb[i][:, BIAS_ON_GPSIMD:E],
-                in0=h_sb[q][:, j, BIAS_ON_GPSIMD:E],
-                in1=b2_upper[:, BIAS_ON_GPSIMD - BANK : BANK],
-                op=ALU.add,
-            )
+        def add_bias(m):
+            hb[m] = biased.tile([P, PAIR, E], F32, name="hb")
+            for i in tiles_of(m):
+                if i < BIASED_BY_VECTOR:
+                    place = place_of(i)[1]
+                    for c, b2_bank in enumerate([b2_lower, b2_upper]):
+                        cols = slice(c * BANK, (c + 1) * BANK)
+                        nc.vector.tensor_tensor(
+                            out=hb[m][:, place, cols],
+                            in0=h_sb[m][:, place, cols],
+                            in1=b2_bank[:],
+                            op=ALU.add,
+                        )
+            places = [place_of(i)[1] for i in tiles_of(m) if i >= BIASED_BY_VECTOR]
+            if places:
+                both = slice(places[0], places[-1] + 1)
+                nc.gpsimd.tensor_tensor(
+                    out=hb[m][:, both, :],
+                    in0=h_sb[m][:, both, :],
+                    in1=b2_sb[:].unsqueeze(1).to_broadcast([P, len(places), E]),
+                    op=ALU.add,
+                )
 
         def add_residual(i):
+            m, place = place_of(i)
             r[i] = work.tile([P, E], F32, name="r")
             sums[i] = stats.tile([P, HALVES], F32, name="sums")
             for c in range(HALVES):
                 cols = slice(c * BANK, (c + 1) * BANK)
                 nc.vector.scalar_tensor_tensor(
                     out=r[i][:, cols],
-                    in0=hb[i][:, cols],
+                    in0=hb[m][:, place, cols],
                     scalar=1.0,
                     in1=mm[i][c][:],
                     op0=ALU.mult,
@@ -305,16 +308,19 @@ def tile_transformerblock_pb_t_kernel(tc, y_act, h, W2_words, W2_scales, b2, g2,
             if first_tile % PAIR == 0 and 0 <= first_tile < N_TILES:
                 stage(first_tile // PAIR)
 
+        def for_couple(stage, even_tile):
+            if even_tile % PAIR == 0 and 0 <= even_tile // PAIR < N_COUPLES:
+                stage(even_tile // PAIR)
+
         def step(t):
-            for_pair(load_pair, t + LOAD_LEAD)
+            for_pair(load_y, t + LOAD_LEAD)
+            for_couple(load_h, t + LOAD_LEAD)
             for_pair(transpose_pair, t + TRANSPOSE_LEAD)
             for_pair(group_pair, t + GROUP_LEAD)
             for_tile(multiply, t + MULTIPLY_LEAD)
             for_tile(add_residual, t)
             for_pair(quantise_pair, t + QUANTISE_LEAD)
-            if t % PAIR == 0:
-                for lead in BIAS_LEADS:
-                    for_tile(add_bias, t + lead)
+            for_couple(add_bias, t + BIAS_LEAD)
             for_tile(centre_and_gain, t - GAIN_LAG)
             for_tile(squares, t - SQUARES_LAG)
             for_tile(scale_and_store, t - SCALE_LAG)
@@ -323,9 +329,5 @@ def tile_transformerblock_pb_t_kernel(tc, y_act, h, W2_words, W2_scales, b2, g2,
 
         step(FIRST_STEP)
         spread_over_partitions(g2_rows, [g2_ps[:, c * BANK : (c + 1) * BANK] for c in range(HALVES)])
-        step(FIRST_STEP + 1)
-        nc.scalar.copy(
-            out=b2_sb[:, BANK:BIAS_ON_GPSIMD], in_=b2_upper[:, 0 : BIAS_ON_GPSIMD - BANK]
-        )
-        for t in range(FIRST_STEP + 2, LAST_STEP + 1):
+        for t in range(FIRST_STEP + 1, LAST_STEP + 1):
             step(t)

@@ -26,6 +26,7 @@ SCALED_BY_GPSIMD = range(LAST_TILE - 4, LAST_TILE)
 EPS = 1e-5
 
 N_COUPLES = N_TILES // PAIR + 1
+COPY_TURN = 4
 BIASED_BY_VECTOR = 2
 
 LOAD_LEAD = 10
@@ -165,7 +166,8 @@ def tile_transformerblock_pb_t_kernel(tc, y_act, h, W2_words, W2_scales, b2, g2,
 
         def group_pair(q):
             grouped[q] = quant.tile([P, PAIR * P * 4], BF16, name="grouped", align_bytes=64)
-            nc.scalar.copy(
+            copy = nc.vector.tensor_copy if q % COPY_TURN == COPY_TURN - 1 else nc.scalar.copy
+            copy(
                 out=grouped[q][:].bitcast(F32).rearrange("p (j i u) -> p j i u", j=PAIR, u=2),
                 in_=y_t[q][:].rearrange("p j u i -> p j i u"),
             )

from contextlib import ExitStack

import concourse.mybir as mybir
from concourse.masks import make_identity

F32 = mybir.dt.float32
BF16 = mybir.dt.bfloat16
I32 = mybir.dt.int32
U32 = mybir.dt.uint32
U8 = mybir.dt.uint8
FP8X4 = mybir.dt.float8_e4m3fn_x4
FP4X4 = mybir.dt.float4_e2m1fn_x4
ALU = mybir.AluOpType
ACT = mybir.ActivationFunctionType

P = 128
TOKENS = 4096
K = 512
E = 1024
BANK = 512
HALVES = E // BANK
PAIR = 2
N_TILES = TOKENS // P
LAST_TILE = N_TILES - 1
SCALED_BY_GPSIMD = range(LAST_TILE - 4, LAST_TILE)
EPS = 1e-5

N_COUPLES = N_TILES // PAIR + 1
COPY_TURN = 4
BIASED_BY_VECTOR = 2

LOAD_LEAD = 10
TRANSPOSE_LEAD = 4
GROUP_LEAD = 3
QUANTISE_LEAD = 2
BIAS_LEAD = 4
MULTIPLY_LEAD = 1
GAIN_LAG = 1
SQUARES_LAG = 1
SCALE_LAG = 2
FIRST_STEP = -TRANSPOSE_LEAD
LAST_STEP = N_TILES - 1 + SCALE_LAG

LOAD_BUFS = LOAD_LEAD // PAIR
QUANT_BUFS = 2
WORK_BUFS = 6
BIAS_BUFS = 2

FLOPS = 2 * TOKENS * K * E


def tile_transformerblock_pb_t_kernel(tc, y_act, h, W2_words, W2_scales, b2, g2, out):
    nc = tc.nc

    y_pairs = y_act.flatten_outer_dims().rearrange("(q p j) k -> q p j k", p=P, j=PAIR)
    h_pairs = h.flatten_outer_dims().rearrange("(q p j) e -> q p j e", p=P, j=PAIR)
    out_pairs = out.flatten_outer_dims().rearrange("(q p j) e -> q p j e", p=P, j=PAIR)

    with ExitStack() as ctx:
        ctx.enter_context(tc.manual_schedule())
        const = ctx.enter_context(tc.tile_pool(name="const", bufs=1))
        loads = ctx.enter_context(tc.tile_pool(name="loads", bufs=LOAD_BUFS))
        quant = ctx.enter_context(tc.tile_pool(name="quant", bufs=QUANT_BUFS))
        work = ctx.enter_context(tc.tile_pool(name="work", bufs=WORK_BUFS))
        stats = ctx.enter_context(tc.tile_pool(name="stats", bufs=WORK_BUFS))
        biased = ctx.enter_context(tc.tile_pool(name="biased", bufs=BIAS_BUFS))
        psum_g2 = ctx.enter_context(tc.psum_pool(name="psum_g2", bufs=1))
        psum_b2 = ctx.enter_context(tc.psum_pool(name="psum_b2", bufs=1))
        psum_yt = ctx.enter_context(tc.psum_pool(name="psum_yt", bufs=1))
        psum_mm = ctx.enter_context(tc.psum_pool(name="psum_mm", bufs=2))

        b2_rows = const.tile([P, E], BF16)
        g2_rows = const.tile([P, E], BF16)
        w_scales = const.tile([P, E], U8, align_bytes=64)
        w_words = const.tile([P, 2 * E], U8, align_bytes=64)
        ones = const.tile([P, P], BF16)
        eps = const.tile([P, 1], F32)
        table_warm = const.tile([P, 1], F32)
        ident = const.tile([P, P], F32)
        b2_sb = const.tile([P, E], F32)

        nc.vector.memset(b2_rows[:].bitcast(I32), 0)
        nc.vector.memset(w_scales[:].bitcast(I32), 0)
        nc.vector.memset(eps[:], EPS)
        nc.vector.memset(ones[:], 1.0)
        nc.vector.memset(g2_rows[:].bitcast(I32), 0)
        make_identity(nc, ident[:])

        nc.scalar.dma_start(out=b2_rows[0:1, :], in_=b2.unsqueeze(0))
        nc.scalar.activation(out=table_warm[:], in_=eps[:], func=ACT.Abs_reciprocal_sqrt)
        nc.scalar.dma_start(out=g2_rows[0:1, :], in_=g2.unsqueeze(0))

        y_sb = {}
        h_sb = {}

        def load_y(q):
            y_sb[q] = loads.tile([P, PAIR, K], BF16, name="y_sb")
            nc.sync.dma_start(out=y_sb[q][:], in_=y_pairs[q])

        def place_of(i):
            return divmod(i + 1, PAIR)

        def tiles_of(m):
            return [i for i in (PAIR * m - 1, PAIR * m) if 0 <= i < N_TILES]

        def load_h(m):
            h_sb[m] = loads.tile([P, PAIR, E], BF16, name="h_sb")
            for i in tiles_of(m):
                q, j = divmod(i, PAIR)
                nc.sync.dma_start(out=h_sb[m][:, place_of(i)[1], :], in_=h_pairs[q][:, j, :])

        load_y(0)
        for quadrant in range(4):
            nc.sync.dma_start(
                out=w_scales[32 * quadrant : 32 * quadrant + 4, :].bitcast(I32),
                in_=W2_scales[0, 4 * quadrant : 4 * quadrant + 4, :].bitcast(I32),
            )
        nc.sync.dma_start(out=w_words[:].bitcast(I32), in_=W2_words[0].bitcast(I32))
        load_h(0)
        load_h(1)
        load_y(1)
        load_y(2)
        load_h(2)

        def spread_over_partitions(rows, banks):
            for c in range(HALVES):
                nc.tensor.matmul(
                    out=banks[c],
                    lhsT=ones[:],
                    rhs=rows[:, c * BANK : (c + 1) * BANK],
                    start=True,
                    stop=True,
                )

        b2_lower = psum_mm.tile([P, BANK], F32, name="mm0")
        b2_upper = psum_b2.tile([P, BANK], F32)
        spread_over_partitions(b2_rows, [b2_lower[:], b2_upper[:]])
        nc.scalar.copy(out=b2_sb[:, 0:BANK], in_=b2_lower[:])
        nc.scalar.copy(out=b2_sb[:, BANK:E], in_=b2_upper[:])
        g2_ps = psum_g2.tile([P, E], BF16, name="g2_ps")

        y_t = {}
        grouped = {}
        y_codes = {}
        y_scales = {}
        mm = {}
        hb = {}
        r = {}
        z = {}
        sums = {}
        neg_mean = {}
        ssq = {}
        rstd = {}

        def transpose_pair(q):
            y_t[q] = psum_yt.tile([P, PAIR, 2, P], F32, name="y_t")
            words = y_sb[q][:].rearrange("p j k -> p (j k)").bitcast(F32)
            for j in range(PAIR):
                for u in range(2):
                    first = j * (K // 2) + u
                    nc.tensor.transpose(
                        out=y_t[q][:, j, u, :],
                        in_=words[:, first : (j + 1) * (K // 2) : 2],
                        identity=ident[:],
                    )

        def group_pair(q):
            grouped[q] = quant.tile([P, PAIR * P * 4], BF16, name="grouped", align_bytes=64)
            copy = nc.vector.tensor_copy if q % COPY_TURN == COPY_TURN - 1 else nc.scalar.copy
            copy(
                out=grouped[q][:].bitcast(F32).rearrange("p (j i u) -> p j i u", j=PAIR, u=2),
                in_=y_t[q][:].rearrange("p j u i -> p j i u"),
            )

        def quantise_pair(q):
            y_codes[q] = quant.tile([P, PAIR * P], U32, name="y_codes", align_bytes=64)
            y_scales[q] = quant.tile([P, PAIR * P], U8, name="y_scales", align_bytes=64)
            nc.vector.quantize_mx(
                out=y_codes[q][:].bitcast(FP8X4), scales=y_scales[q][:], in_=grouped[q][:]
            )

        def multiply(i):
            q, j = divmod(i, PAIR)
            tokens = slice(j * P, (j + 1) * P)
            mm[i] = [psum_mm.tile([P, BANK], F32, name="mm%d" % c) for c in range(HALVES)]
            for c in range(HALVES):
                nc.tensor.matmul_mx(
                    out=mm[i][c][:],
                    lhsT=y_codes[q][:, tokens].bitcast(FP8X4),
                    lhsT_scale=y_scales[q][:, tokens],
                    rhs=w_words[:, c * 2 * BANK : (c + 1) * 2 * BANK].bitcast(FP4X4),
                    rhs_scale=w_scales[:, c * BANK : (c + 1) * BANK],
                    start=True,
                    stop=True,
                )

        def add_bias(m):
            hb[m] = biased.tile([P, PAIR, E], F32, name="hb")
            for i in tiles_of(m):
                if i < BIASED_BY_VECTOR:
                    place = place_of(i)[1]
                    for c, b2_bank in enumerate([b2_lower, b2_upper]):
                        cols = slice(c * BANK, (c + 1) * BANK)
                        nc.vector.tensor_tensor(
                            out=hb[m][:, place, cols],
                            in0=h_sb[m][:, place, cols],
                            in1=b2_bank[:],
                            op=ALU.add,
                        )
            places = [place_of(i)[1] for i in tiles_of(m) if i >= BIASED_BY_VECTOR]
            if places:
                both = slice(places[0], places[-1] + 1)
                nc.gpsimd.tensor_tensor(
                    out=hb[m][:, both, :],
                    in0=h_sb[m][:, both, :],
                    in1=b2_sb[:].unsqueeze(1).to_broadcast([P, len(places), E]),
                    op=ALU.add,
                )

        def add_residual(i):
            m, place = place_of(i)
            r[i] = work.tile([P, E], F32, name="r")
            sums[i] = stats.tile([P, HALVES], F32, name="sums")
            for c in range(HALVES):
                cols = slice(c * BANK, (c + 1) * BANK)
                nc.vector.scalar_tensor_tensor(
                    out=r[i][:, cols],
                    in0=hb[m][:, place, cols],
                    scalar=1.0,
                    in1=mm[i][c][:],
                    op0=ALU.mult,
                    op1=ALU.add,
                    accum_out=sums[i][:, c : c + 1],
                )

        def mean(i):
            scaled_sums = stats.tile([P, HALVES], F32, name="scaled_sums")
            neg_mean[i] = stats.tile([P, 1], F32, name="neg_mean")
            nc.scalar.activation(
                out=scaled_sums[:],
                in_=sums[i][:],
                func=ACT.Copy,
                scale=-1.0 / E,
                accum_out=neg_mean[i][:],
            )

        def squares(i):
            scratch = work.tile([P, E], BF16, name="scratch")
            ssq[i] = stats.tile([P, 1], F32, name="ssq")
            nc.scalar.activation(
                out=scratch[:],
                in_=r[i][:],
                func=ACT.Square,
                bias=neg_mean[i][:, 0:1],
                scale=1.0,
                accum_out=ssq[i][:],
            )

        def pieces_of(i):
            if i == LAST_TILE:
                return [slice(c * BANK, (c + 1) * BANK) for c in range(HALVES)]
            return [slice(0, E)]

        def centre_and_gain(i):
            z[i] = work.tile([P, E], F32, name="z")
            for cols in pieces_of(i):
                nc.vector.scalar_tensor_tensor(
                    out=z[i][:, cols],
                    in0=r[i][:, cols],
                    scalar=neg_mean[i][:, 0:1],
                    in1=g2_ps[:, cols],
                    op0=ALU.add,
                    op1=ALU.mult,
                )

        def inverse_std(i):
            rstd[i] = stats.tile([P, 1], F32, name="rstd")
            nc.scalar.activation(
                out=rstd[i][:],
                in_=ssq[i][:],
                func=ACT.Abs_reciprocal_sqrt,
                bias=eps[:, 0:1],
                scale=1.0 / E,
            )

        def scale_and_store(i):
            q, j = divmod(i, PAIR)
            if i in SCALED_BY_GPSIMD:
                nc.gpsimd.tensor_scalar(
                    out=z[i][:],
                    in0=z[i][:],
                    scalar1=rstd[i][:, 0:1],
                    scalar2=0.0,
                    op0=ALU.mult,
                    op1=ALU.add,
                )
                nc.sync.dma_start(out=out_pairs[q][:, j, :], in_=z[i][:])
                return
            for cols in pieces_of(i):
                nc.scalar.activation(
                    out=z[i][:, cols], in_=z[i][:, cols], func=ACT.Copy, scale=rstd[i][:, 0:1]
                )
                nc.sync.dma_start(out=out_pairs[q][:, j, cols], in_=z[i][:, cols])

        def for_tile(stage, i):
            if 0 <= i < N_TILES:
                stage(i)

        def for_pair(stage, first_tile):
            if first_tile % PAIR == 0 and 0 <= first_tile < N_TILES:
                stage(first_tile // PAIR)

        def for_couple(stage, even_tile):
            if even_tile % PAIR == 0 and 0 <= even_tile // PAIR < N_COUPLES:
                stage(even_tile // PAIR)

        def step(t):
            for_pair(load_y, t + LOAD_LEAD)
            for_couple(load_h, t + LOAD_LEAD)
            for_pair(transpose_pair, t + TRANSPOSE_LEAD)
            for_pair(group_pair, t + GROUP_LEAD)
            for_tile(multiply, t + MULTIPLY_LEAD)
            for_tile(add_residual, t)
            for_pair(quantise_pair, t + QUANTISE_LEAD)
            for_couple(add_bias, t + BIAS_LEAD)
            for_tile(centre_and_gain, t - GAIN_LAG)
            for_tile(squares, t - SQUARES_LAG)
            for_tile(scale_and_store, t - SCALE_LAG)
            for_tile(inverse_std, t - SQUARES_LAG)
            for_tile(mean, t)

        step(FIRST_STEP)
        spread_over_partitions(g2_rows, [g2_ps[:, c * BANK : (c + 1) * BANK] for c in range(HALVES)])
        for t in range(FIRST_STEP + 1, LAST_STEP + 1):
            step(t)
